import numpy as np
import ml_dtypes


def mxq(x, axis, fmt="e4m3"):
    dtype, down = {"e4m3": (ml_dtypes.float8_e4m3fn, 7), "e5m2": (ml_dtypes.float8_e5m2, 14)}[fmt]
    v = np.moveaxis(np.asarray(x, np.float32).astype(ml_dtypes.bfloat16).astype(np.float64), axis, -1)
    blocks = v.reshape(v.shape[:-1] + (-1, 32))
    amax = np.abs(blocks).max(-1, keepdims=True)
    byte = np.maximum(np.where(amax > 0, np.frexp(amax)[1] - 1 + 127, 0) - down, 1)
    scale = np.exp2(byte - 127.0)
    codes = (blocks / scale).astype(np.float32).astype(dtype).astype(np.float64)
    return np.moveaxis((codes * scale).reshape(v.shape), -1, axis)


WIDE = False


def mx_kscale(k):
    if not WIDE:
        return np.ones(k)
    levels = np.array([10, -10, 5, -5, 0])
    a = np.random.permutation(np.resize(levels, k // 512 * 4)).reshape(k // 512, 4)
    idx = np.arange(k)
    return np.exp2(a[idx // 512, idx % 128 // 32])


BF16 = ml_dtypes.bfloat16


def bf(x):
    return np.asarray(x, np.float32).astype(BF16)


def f64(x):
    return np.asarray(x).astype(np.float64)


B, N, P, D, H = 2, 512, 4, 256, 8
E = P * D
DH = E // H
SIG = np.sqrt(DH / (D // H))


def setup_inputs():
    s, t = mx_kscale(N), mx_kscale(E)
    z = np.random.standard_normal((B, H, N, N)) * SIG
    z = np.exp(z - z.max(-1, keepdims=True))
    return {"attn_weights": bf(z / z.sum(-1, keepdims=True) * s),
            "v": bf(np.random.standard_normal((B, N, H, DH)) * t.reshape(H, DH) / s[:, None, None]),
            "Wo": bf(np.random.standard_normal((E, E)) * 3.0 / np.sqrt(E) / t),
            "bo": bf(np.random.standard_normal(E) * 0.1)}


def reference(attn_weights, v, Wo, bo):
    o = mxq(f64(attn_weights), 3, "e4m3") @ mxq(f64(v).transpose(0, 2, 1, 3), 2, "e4m3")
    o = o.transpose(0, 2, 1, 3).reshape(B, N, E)
    out = (mxq(o, 2, "e4m3") @ mxq(f64(Wo).T, 0, "e4m3")) + f64(bo)
    return out.reshape(B, N, P, D)

@@ -1,0 +1,240 @@
+from contextlib import ExitStack
+
+import concourse.mybir as mybir
+from concourse.masks import make_identity
+
+BF16 = mybir.dt.bfloat16
+F32 = mybir.dt.float32
+U32 = mybir.dt.uint32
+U8 = mybir.dt.uint8
+FP8X4 = mybir.dt.float8_e4m3fn_x4
+
+P = 128
+PACK = 4
+BATCHES = 2
+TOKENS = 512
+HEADS = 8
+FEATURES = HEADS * P
+BANK = 512
+PASSES = FEATURES // (P * PACK)
+HALVES = FEATURES // BANK
+ROWS_PER_PARTITION = 2
+UNIT_TOKENS = ROWS_PER_PARTITION * P
+UNITS = BATCHES * TOKENS // UNIT_TOKENS
+STEPS = UNITS * ROWS_PER_PARTITION
+
+FLOPS = 2 * BATCHES * HEADS * TOKENS * TOKENS * P + 2 * BATCHES * TOKENS * FEATURES * FEATURES
+
+
+def tile_attention_pb_kernel(tc, attn_weights, v, Wo, bo, out):
+    nc = tc.nc
+    with ExitStack() as ctx:
+        keep = ctx.enter_context(tc.tile_pool(name="keep", bufs=1))
+        ring = ctx.enter_context(tc.tile_pool(name="ring", bufs=2))
+        psum_turn = ctx.enter_context(tc.psum_pool(name="psum_turn", bufs=4))
+        psum_mix = ctx.enter_context(tc.psum_pool(name="psum_mix", bufs=2))
+        psum_out = ctx.enter_context(tc.psum_pool(name="psum_out", bufs=2))
+        ctx.enter_context(tc.manual_schedule())
+
+        ident_f32 = keep.tile([P, P], F32, name="ident_f32")
+        make_identity(nc, ident_f32[:])
+        ident_bf16 = keep.tile([P, P], BF16, name="ident_bf16")
+        make_identity(nc, ident_bf16[:])
+        ones = keep.tile([P, P], BF16, name="ones")
+        nc.vector.memset(ones[:], 1.0)
+        bias_rows = keep.tile([P, FEATURES], BF16, name="bias_rows")
+        nc.vector.memset(bias_rows[:], 0.0)
+
+        nc.scalar.dma_start(out=bias_rows[0:1, :], in_=bo.rearrange("(o e) -> o e", o=1))
+
+        def load_wo(pair):
+            raw = keep.tile([P, 2, FEATURES], BF16, name="wo_raw%d" % pair)
+            rows = Wo[2 * P * pair : 2 * P * (pair + 1), :]
+            nc.sync.dma_start(out=raw[:], in_=rows.rearrange("(r p) e -> p r e", p=P))
+            return raw
+
+        def load_v(b):
+            raw = keep.tile([P, PACK, FEATURES], BF16, name="v_raw%d" % b)
+            nc.sync.dma_start(
+                out=raw[:].rearrange("p (u e) c -> p u e c", u=2),
+                in_=v[b].rearrange("(u p e) h d -> p u e (h d)", u=2, e=2),
+            )
+            return raw
+
+        def load_attn(unit, g):
+            b, part = divmod(unit, UNITS // BATCHES)
+            raw = keep.tile([P, PACK, ROWS_PER_PARTITION, TOKENS], BF16, name="a_raw%d_%d" % (unit, g))
+            rows = attn_weights[b, PACK * g : PACK * (g + 1), UNIT_TOKENS * part : UNIT_TOKENS * (part + 1), :]
+            nc.sync.dma_start(out=raw[:], in_=rows.rearrange("h (p j) k -> p h j k", j=ROWS_PER_PARTITION))
+            return raw
+
+        wo_raw = [load_wo(0), load_wo(1)]
+        v_raw = [load_v(0)]
+        wo_raw.extend([load_wo(2), load_wo(3)])
+        a_raw = {}
+        for g in range(PASSES):
+            a_raw[(0, g)] = load_attn(0, g)
+        v_raw.append(load_v(1))
+        for unit in range(1, UNITS):
+            for g in range(PASSES):
+                a_raw[(unit, g)] = load_attn(unit, g)
+
+        v_codes = []
+        v_scales = []
+
+        def prepare_v(b):
+            grouped = keep.tile([P, FEATURES, PACK], BF16, name="v_grouped", align_bytes=64)
+            codes = keep.tile([P, FEATURES], U32, name="v_codes%d" % b, align_bytes=64)
+            scales = keep.tile([P, FEATURES], U8, name="v_scales%d" % b, align_bytes=64)
+            halves = [slice(BANK * s, BANK * (s + 1)) for s in range(HALVES)]
+            for cols in halves:
+                nc.vector.tensor_copy(
+                    out=grouped[:, cols, :].rearrange("p (c i) t -> p c t i", i=4),
+                    in_=v_raw[b][:, :, cols].rearrange("p t (c i) -> p c t i", i=4),
+                )
+            for cols in halves:
+                nc.vector.quantize_mx(
+                    out=codes[:, cols].bitcast(FP8X4),
+                    scales=scales[:, cols],
+                    in_=grouped[:, cols, :].rearrange("p c t -> p (c t)"),
+                )
+            v_codes.append(codes)
+            v_scales.append(scales)
+
+        prepare_v(0)
+
+        wo_codes = []
+        wo_scales = []
+        for half in range(HALVES):
+            grouped = ring.tile([P, PASSES, BANK, PACK], BF16, name="wo_grouped", align_bytes=64)
+            for block in range(BANK // P):
+                raw = wo_raw[2 * half + block // 2][:, block % 2, :]
+                for g in range(PASSES):
+                    turned = psum_turn.tile([P, PACK, P], BF16, name="wo_turned", tag="turned")
+                    for t in range(PACK):
+                        first = P * (PACK * g + t)
+                        nc.tensor.transpose(turned[:, t, :], raw[:, first : first + P], ident_bf16[:])
+                    nc.scalar.copy(
+                        out=grouped[:, g, P * block : P * (block + 1), :],
+                        in_=turned[:].rearrange("p t f -> p f t"),
+                    )
+            codes = keep.tile([P, PASSES * BANK], U32, name="wo_codes%d" % half, align_bytes=64)
+            scales = keep.tile([P, PASSES * BANK], U8, name="wo_scales%d" % half, align_bytes=64)
+            nc.vector.quantize_mx(
+                out=codes[:].bitcast(FP8X4),
+                scales=scales[:],
+                in_=grouped[:].rearrange("p g f t -> p (g f t)"),
+            )
+            wo_codes.append(codes)
+            wo_scales.append(scales)
+
+        bias = keep.tile([P, FEATURES], F32, name="bias")
+        for half in range(HALVES):
+            cols = slice(BANK * half, BANK * (half + 1))
+            spread = psum_out.tile([P, BANK], F32, name="spread", tag="acc")
+            nc.tensor.matmul(out=spread[:], lhsT=ones[:], rhs=bias_rows[:, cols], start=True, stop=True)
+            nc.vector.tensor_copy(out=bias[:, cols], in_=spread[:])
+
+        prepare_v(1)
+
+        a_grouped = {}
+        a_codes = {}
+        a_scales = {}
+        mixed = {}
+        o_codes = {}
+        o_scales = {}
+
+        def turn(step):
+            unit, j = divmod(step, ROWS_PER_PARTITION)
+            grouped = ring.tile([P, HEADS * P * PACK], BF16, name="a_grouped", align_bytes=64)
+            for pair in range(HEADS // 2):
+                turned = psum_turn.tile([P, 2, 2, P], F32, name="a_turned", tag="turned")
+                for i in range(2):
+                    g, t = divmod(2 * pair + i, PACK)
+                    words = a_raw[(unit, g)][:, t, j, :].bitcast(F32)
+                    for u in range(2):
+                        nc.tensor.transpose(turned[:, i, u, :], words[:, P * u : P * (u + 1)], ident_f32[:])
+                width = 2 * P * PACK
+                nc.scalar.copy(
+                    out=grouped[:, width * pair : width * (pair + 1)]
+                    .bitcast(F32)
+                    .rearrange("p (i n u) -> p i n u", i=2, u=2),
+                    in_=turned[:].rearrange("p i u n -> p i n u"),
+                )
+            a_grouped[step] = grouped
+
+        def quantise_attn(step):
+            codes = ring.tile([P, HEADS * P], U32, name="a_codes", align_bytes=64)
+            scales = ring.tile([P, HEADS * P], U8, name="a_scales", align_bytes=64)
+            nc.vector.quantize_mx(out=codes[:].bitcast(FP8X4), scales=scales[:], in_=a_grouped[step][:])
+            a_codes[step] = codes
+            a_scales[step] = scales
+
+        def mix(step):
+            b = step // (STEPS // BATCHES)
+            banks = []
+            for g in range(PASSES):
+                bank = psum_mix.tile([P, PACK, P], F32, name="o_turned")
+                for t in range(PACK):
+                    cols = slice(P * (PACK * g + t), P * (PACK * g + t + 1))
+                    nc.tensor.matmul_mx(
+                        out=bank[:, t, :],
+                        lhsT=v_codes[b][:, cols].bitcast(FP8X4),
+                        lhsT_scale=v_scales[b][:, cols],
+                        rhs=a_codes[step][:, cols].bitcast(FP8X4),
+                        rhs_scale=a_scales[step][:, cols],
+                        start=True,
+                        stop=True,
+                    )
+                banks.append(bank)
+            mixed[step] = banks
+
+        def quantise_mixed(step):
+            grouped = ring.tile([P, PASSES, P, PACK], BF16, name="o_grouped", align_bytes=64)
+            nc.scalar.copy(out=grouped[:, 0, :, :], in_=mixed[step][0][:].rearrange("p t n -> p n t"))
+            nc.vector.tensor_copy(out=grouped[:, 1, :, :], in_=mixed[step][1][:].rearrange("p t n -> p n t"))
+            codes = ring.tile([P, PASSES * P], U32, name="o_codes", align_bytes=64)
+            scales = ring.tile([P, PASSES * P], U8, name="o_scales", align_bytes=64)
+            nc.vector.quantize_mx(
+                out=codes[:].bitcast(FP8X4),
+                scales=scales[:],
+                in_=grouped[:].rearrange("p g n t -> p (g n t)"),
+            )
+            o_codes[step] = codes
+            o_scales[step] = scales
+
+        def project(step):
+            unit, j = divmod(step, ROWS_PER_PARTITION)
+            b, part = divmod(unit, UNITS // BATCHES)
+            result = keep.tile([P, FEATURES], F32, name="result%d" % step)
+            for half in range(HALVES):
+                acc = psum_out.tile([P, BANK], F32, name="acc", tag="acc")
+                for g in range(PASSES):
+                    nc.tensor.matmul_mx(
+                        out=acc[:],
+                        lhsT=o_codes[step][:, P * g : P * (g + 1)].bitcast(FP8X4),
+                        lhsT_scale=o_scales[step][:, P * g : P * (g + 1)],
+                        rhs=wo_codes[half][:, BANK * g : BANK * (g + 1)].bitcast(FP8X4),
+                        rhs_scale=wo_scales[half][:, BANK * g : BANK * (g + 1)],
+                        start=(g == 0),
+                        stop=(g == PASSES - 1),
+                    )
+                cols = slice(BANK * half, BANK * (half + 1))
+                nc.vector.tensor_tensor(out=result[:, cols], in0=acc[:], in1=bias[:, cols], op=mybir.AluOpType.add)
+            rows = out[b, UNIT_TOKENS * part : UNIT_TOKENS * (part + 1)]
+            nc.sync.dma_start(
+                out=rows.rearrange("(p j) a d -> p j (a d)", j=ROWS_PER_PARTITION)[:, j, :],
+                in_=result[:],
+            )
+
+        for i in range(STEPS + 2):
+            if i >= 2:
+                quantise_mixed(i - 2)
+            if i < STEPS:
+                turn(i)
+            if 1 <= i <= STEPS:
+                quantise_attn(i - 1)
+            if i >= 2:
+                project(i - 2)
+            if 1 <= i <= STEPS:
+                mix(i - 1)

@@ -82,26 +82,32 @@ def tile_attention_pb_kernel(tc, attn_weights, v, Wo, bo, out):
         v_codes = []
         v_scales = []
 
-        def prepare_v(b):
+        v_grouped = []
+        halves = [slice(BANK * s, BANK * (s + 1)) for s in range(HALVES)]
+
+        def regroup_v(b):
             grouped = keep.tile([P, FEATURES, PACK], BF16, name="v_grouped", align_bytes=64)
-            codes = keep.tile([P, FEATURES], U32, name="v_codes%d" % b, align_bytes=64)
-            scales = keep.tile([P, FEATURES], U8, name="v_scales%d" % b, align_bytes=64)
-            halves = [slice(BANK * s, BANK * (s + 1)) for s in range(HALVES)]
             for cols in halves:
                 nc.vector.tensor_copy(
                     out=grouped[:, cols, :].rearrange("p (c i) t -> p c t i", i=4),
                     in_=v_raw[b][:, :, cols].rearrange("p t (c i) -> p c t i", i=4),
                 )
+            v_grouped.append(grouped)
+
+        def quantise_v(b):
+            codes = keep.tile([P, FEATURES], U32, name="v_codes%d" % b, align_bytes=64)
+            scales = keep.tile([P, FEATURES], U8, name="v_scales%d" % b, align_bytes=64)
             for cols in halves:
                 nc.vector.quantize_mx(
                     out=codes[:, cols].bitcast(FP8X4),
                     scales=scales[:, cols],
-                    in_=grouped[:, cols, :].rearrange("p c t -> p (c t)"),
+                    in_=v_grouped[b][:, cols, :].rearrange("p c t -> p (c t)"),
                 )
             v_codes.append(codes)
             v_scales.append(scales)
 
-        prepare_v(0)
+        regroup_v(0)
+        quantise_v(0)
 
         wo_codes = []
         wo_scales = []
@@ -135,12 +141,11 @@ def tile_attention_pb_kernel(tc, attn_weights, v, Wo, bo, out):
             nc.tensor.matmul(out=spread[:], lhsT=ones[:], rhs=bias_rows[:, cols], start=True, stop=True)
             nc.vector.tensor_copy(out=bias[:, cols], in_=spread[:])
 
-        prepare_v(1)
-
         a_grouped = {}
         a_codes = {}
         a_scales = {}
         mixed = {}
+        o_grouped = {}
         o_codes = {}
         o_scales = {}
 
@@ -166,7 +171,13 @@ def tile_attention_pb_kernel(tc, attn_weights, v, Wo, bo, out):
         def quantise_attn(step):
             codes = ring.tile([P, HEADS * P], U32, name="a_codes", align_bytes=64)
             scales = ring.tile([P, HEADS * P], U8, name="a_scales", align_bytes=64)
-            nc.vector.quantize_mx(out=codes[:].bitcast(FP8X4), scales=scales[:], in_=a_grouped[step][:])
+            for g in range(PASSES):
+                cols = slice(PACK * P * g, PACK * P * (g + 1))
+                nc.vector.quantize_mx(
+                    out=codes[:, cols].bitcast(FP8X4),
+                    scales=scales[:, cols],
+                    in_=a_grouped[step][:, PACK * PACK * P * g : PACK * PACK * P * (g + 1)],
+                )
             a_codes[step] = codes
             a_scales[step] = scales
 
@@ -189,16 +200,19 @@ def tile_attention_pb_kernel(tc, attn_weights, v, Wo, bo, out):
                 banks.append(bank)
             mixed[step] = banks
 
-        def quantise_mixed(step):
+        def round_mixed(step):
             grouped = ring.tile([P, PASSES, P, PACK], BF16, name="o_grouped", align_bytes=64)
-            nc.scalar.copy(out=grouped[:, 0, :, :], in_=mixed[step][0][:].rearrange("p t n -> p n t"))
-            nc.vector.tensor_copy(out=grouped[:, 1, :, :], in_=mixed[step][1][:].rearrange("p t n -> p n t"))
+            for g in range(PASSES):
+                nc.scalar.copy(out=grouped[:, g, :, :], in_=mixed[step][g][:].rearrange("p t n -> p n t"))
+            o_grouped[step] = grouped
+
+        def quantise_mixed(step):
             codes = ring.tile([P, PASSES * P], U32, name="o_codes", align_bytes=64)
             scales = ring.tile([P, PASSES * P], U8, name="o_scales", align_bytes=64)
             nc.vector.quantize_mx(
                 out=codes[:].bitcast(FP8X4),
                 scales=scales[:],
-                in_=grouped[:].rearrange("p g n t -> p (g n t)"),
+                in_=o_grouped[step][:].rearrange("p g n t -> p (g n t)"),
             )
             o_codes[step] = codes
             o_scales[step] = scales
@@ -206,6 +220,8 @@ def tile_attention_pb_kernel(tc, attn_weights, v, Wo, bo, out):
         def project(step):
             unit, j = divmod(step, ROWS_PER_PARTITION)
             b, part = divmod(unit, UNITS // BATCHES)
+            rows = out[b, UNIT_TOKENS * part : UNIT_TOKENS * (part + 1)]
+            rows = rows.rearrange("(p j) a d -> p j (a d)", j=ROWS_PER_PARTITION)[:, j, :]
             result = keep.tile([P, FEATURES], F32, name="result%d" % step)
             for half in range(HALVES):
                 acc = psum_out.tile([P, BANK], F32, name="acc", tag="acc")
@@ -221,20 +237,22 @@ def tile_attention_pb_kernel(tc, attn_weights, v, Wo, bo, out):
                     )
                 cols = slice(BANK * half, BANK * (half + 1))
                 nc.vector.tensor_tensor(out=result[:, cols], in0=acc[:], in1=bias[:, cols], op=mybir.AluOpType.add)
-            rows = out[b, UNIT_TOKENS * part : UNIT_TOKENS * (part + 1)]
-            nc.sync.dma_start(
-                out=rows.rearrange("(p j) a d -> p j (a d)", j=ROWS_PER_PARTITION)[:, j, :],
-                in_=result[:],
-            )
+                nc.sync.dma_start(out=rows[:, cols], in_=result[:, cols])
 
-        for i in range(STEPS + 2):
-            if i >= 2:
-                quantise_mixed(i - 2)
+        for i in range(STEPS + 3):
+            if 0 <= i - 2 < STEPS:
+                round_mixed(i - 2)
             if i < STEPS:
                 turn(i)
-            if 1 <= i <= STEPS:
+            if 0 <= i - 1 < STEPS:
                 quantise_attn(i - 1)
-            if i >= 2:
-                project(i - 2)
-            if 1 <= i <= STEPS:
+            if 0 <= i - 2 < STEPS:
+                quantise_mixed(i - 2)
+            if i == 1:
+                regroup_v(1)
+            if i == 2:
+                quantise_v(1)
+            if 0 <= i - 3:
+                project(i - 3)
+            if 0 <= i - 1 < STEPS:
                 mix(i - 1)

@@ -61,23 +61,28 @@ def tile_attention_pb_kernel(tc, attn_weights, v, Wo, bo, out):
             )
             return raw
 
-        def load_attn(unit, g):
-            b, part = divmod(unit, UNITS // BATCHES)
-            raw = keep.tile([P, PACK, ROWS_PER_PARTITION, TOKENS], BF16, name="a_raw%d_%d" % (unit, g))
-            rows = attn_weights[b, PACK * g : PACK * (g + 1), UNIT_TOKENS * part : UNIT_TOKENS * (part + 1), :]
-            nc.sync.dma_start(out=raw[:], in_=rows.rearrange("h (p j) k -> p h j k", j=ROWS_PER_PARTITION))
-            return raw
-
-        wo_raw = [load_wo(0), load_wo(1)]
-        v_raw = [load_v(0)]
-        wo_raw.extend([load_wo(2), load_wo(3)])
         a_raw = {}
+
+        def load_attn(unit, first, heads):
+            b, part = divmod(unit, UNITS // BATCHES)
+            raw = keep.tile([P, heads, ROWS_PER_PARTITION, TOKENS], BF16, name="a_raw%d_%d" % (unit, first))
+            rows = attn_weights[b, first : first + heads, UNIT_TOKENS * part : UNIT_TOKENS * (part + 1), :]
+            nc.sync.dma_start(out=raw[:], in_=rows.rearrange("h (p j) k -> p h j k", j=ROWS_PER_PARTITION))
+            for h in range(heads):
+                a_raw[(unit, first + h)] = raw[:, h, :, :]
+
+        load_attn(0, 0, 2)
+        load_attn(0, 2, 2)
+        v_raw = [load_v(0)]
+        load_attn(0, 4, 2)
+        load_attn(0, 6, 2)
+        wo_raw = [load_wo(pair) for pair in range(FEATURES // (2 * P))]
         for g in range(PASSES):
-            a_raw[(0, g)] = load_attn(0, g)
+            load_attn(1, PACK * g, PACK)
         v_raw.append(load_v(1))
-        for unit in range(1, UNITS):
+        for unit in range(2, UNITS):
             for g in range(PASSES):
-                a_raw[(unit, g)] = load_attn(unit, g)
+                load_attn(unit, PACK * g, PACK)
 
         v_codes = []
         v_scales = []
@@ -106,12 +111,10 @@ def tile_attention_pb_kernel(tc, attn_weights, v, Wo, bo, out):
             v_codes.append(codes)
             v_scales.append(scales)
 
-        regroup_v(0)
-        quantise_v(0)
-
         wo_codes = []
         wo_scales = []
-        for half in range(HALVES):
+
+        def prepare_wo(half):
             grouped = ring.tile([P, PASSES, BANK, PACK], BF16, name="wo_grouped", align_bytes=64)
             for block in range(BANK // P):
                 raw = wo_raw[2 * half + block // 2][:, block % 2, :]
@@ -135,11 +138,13 @@ def tile_attention_pb_kernel(tc, attn_weights, v, Wo, bo, out):
             wo_scales.append(scales)
 
         bias = keep.tile([P, FEATURES], F32, name="bias")
-        for half in range(HALVES):
-            cols = slice(BANK * half, BANK * (half + 1))
-            spread = psum_out.tile([P, BANK], F32, name="spread", tag="acc")
-            nc.tensor.matmul(out=spread[:], lhsT=ones[:], rhs=bias_rows[:, cols], start=True, stop=True)
-            nc.vector.tensor_copy(out=bias[:, cols], in_=spread[:])
+
+        def spread_bias():
+            for half in range(HALVES):
+                cols = slice(BANK * half, BANK * (half + 1))
+                spread = psum_out.tile([P, BANK], F32, name="spread", tag="acc")
+                nc.tensor.matmul(out=spread[:], lhsT=ones[:], rhs=bias_rows[:, cols], start=True, stop=True)
+                nc.vector.tensor_copy(out=bias[:, cols], in_=spread[:])
 
         a_grouped = {}
         a_codes = {}
@@ -149,14 +154,15 @@ def tile_attention_pb_kernel(tc, attn_weights, v, Wo, bo, out):
         o_codes = {}
         o_scales = {}
 
-        def turn(step):
+        def turn(step, pairs):
             unit, j = divmod(step, ROWS_PER_PARTITION)
-            grouped = ring.tile([P, HEADS * P * PACK], BF16, name="a_grouped", align_bytes=64)
-            for pair in range(HEADS // 2):
+            if step not in a_grouped:
+                a_grouped[step] = ring.tile([P, HEADS * P * PACK], BF16, name="a_grouped", align_bytes=64)
+            grouped = a_grouped[step]
+            for pair in pairs:
                 turned = psum_turn.tile([P, 2, 2, P], F32, name="a_turned", tag="turned")
                 for i in range(2):
-                    g, t = divmod(2 * pair + i, PACK)
-                    words = a_raw[(unit, g)][:, t, j, :].bitcast(F32)
+                    words = a_raw[(unit, 2 * pair + i)][:, j, :].bitcast(F32)
                     for u in range(2):
                         nc.tensor.transpose(turned[:, i, u, :], words[:, P * u : P * (u + 1)], ident_f32[:])
                 width = 2 * P * PACK
@@ -166,7 +172,6 @@ def tile_attention_pb_kernel(tc, attn_weights, v, Wo, bo, out):
                     .rearrange("p (i n u) -> p i n u", i=2, u=2),
                     in_=turned[:].rearrange("p i u n -> p i n u"),
                 )
-            a_grouped[step] = grouped
 
         def quantise_attn(step):
             codes = ring.tile([P, HEADS * P], U32, name="a_codes", align_bytes=64)
@@ -239,20 +244,33 @@ def tile_attention_pb_kernel(tc, attn_weights, v, Wo, bo, out):
                 nc.vector.tensor_tensor(out=result[:, cols], in0=acc[:], in1=bias[:, cols], op=mybir.AluOpType.add)
                 nc.sync.dma_start(out=rows[:, cols], in_=result[:, cols])
 
-        for i in range(STEPS + 3):
+        early, late = range(HEADS // 4), range(HEADS // 4, HEADS // 2)
+        for step in range(ROWS_PER_PARTITION):
+            turn(step, early)
+        regroup_v(0)
+        quantise_v(0)
+        for step in range(ROWS_PER_PARTITION):
+            turn(step, late)
+        for step in range(ROWS_PER_PARTITION):
+            quantise_attn(step)
+        prepare_wo(0)
+        spread_bias()
+        prepare_wo(1)
+        mix(0)
+
+        for i in range(ROWS_PER_PARTITION, STEPS + 3):
             if 0 <= i - 2 < STEPS:
                 round_mixed(i - 2)
             if i < STEPS:
-                turn(i)
-            if 0 <= i - 1 < STEPS:
-                quantise_attn(i - 1)
+                turn(i, range(HEADS // 2))
             if 0 <= i - 2 < STEPS:
                 quantise_mixed(i - 2)
-            if i == 1:
-                regroup_v(1)
-            if i == 2:
-                quantise_v(1)
-            if 0 <= i - 3:
-                project(i - 3)
+            if i < STEPS:
+                quantise_attn(i)
             if 0 <= i - 1 < STEPS:
                 mix(i - 1)
+            if 0 <= i - 3:
+                project(i - 3)
+            if i == 3:
+                regroup_v(1)
+                quantise_v(1)

@@ -63,26 +63,38 @@ def tile_attention_pb_kernel(tc, attn_weights, v, Wo, bo, out):
 
         a_raw = {}
 
-        def load_attn(unit, first, heads):
+        def attn_rows(unit, first, heads):
             b, part = divmod(unit, UNITS // BATCHES)
-            raw = keep.tile([P, heads, ROWS_PER_PARTITION, TOKENS], BF16, name="a_raw%d_%d" % (unit, first))
             rows = attn_weights[b, first : first + heads, UNIT_TOKENS * part : UNIT_TOKENS * (part + 1), :]
-            nc.sync.dma_start(out=raw[:], in_=rows.rearrange("h (p j) k -> p h j k", j=ROWS_PER_PARTITION))
-            for h in range(heads):
-                a_raw[(unit, first + h)] = raw[:, h, :, :]
+            return rows.rearrange("h (p j) k -> p h j k", j=ROWS_PER_PARTITION)
 
-        load_attn(0, 0, 2)
-        load_attn(0, 2, 2)
+        def load_unit(unit, first, heads):
+            raw = keep.tile([P, heads, ROWS_PER_PARTITION, TOKENS], BF16, name="a_raw%d_%d" % (unit, first))
+            nc.sync.dma_start(out=raw[:], in_=attn_rows(unit, first, heads))
+            for h in range(heads):
+                for j in range(ROWS_PER_PARTITION):
+                    a_raw[(ROWS_PER_PARTITION * unit + j, first + h)] = raw[:, h, j, :]
+
+        def load_step(step, first, heads):
+            unit, j = divmod(step, ROWS_PER_PARTITION)
+            raw = keep.tile([P, heads, TOKENS], BF16, name="a_step%d_%d" % (step, first))
+            nc.sync.dma_start(out=raw[:], in_=attn_rows(unit, first, heads)[:, :, j, :])
+            for h in range(heads):
+                a_raw[(step, first + h)] = raw[:, h, :]
+
+        wo_raw = [load_wo(0), load_wo(1)]
+        load_unit(0, 0, 2)
+        load_unit(0, 2, 2)
         v_raw = [load_v(0)]
-        load_attn(0, 4, 2)
-        load_attn(0, 6, 2)
-        wo_raw = [load_wo(pair) for pair in range(FEATURES // (2 * P))]
+        load_unit(0, 4, 2)
+        load_unit(0, 6, 2)
+        wo_raw.extend([load_wo(2), load_wo(3)])
         for g in range(PASSES):
-            load_attn(1, PACK * g, PACK)
+            load_unit(1, PACK * g, PACK)
         v_raw.append(load_v(1))
-        for unit in range(2, UNITS):
+        for step in range(STEPS // 2, STEPS):
             for g in range(PASSES):
-                load_attn(unit, PACK * g, PACK)
+                load_step(step, PACK * g, PACK)
 
         v_codes = []
         v_scales = []
@@ -123,7 +135,8 @@ def tile_attention_pb_kernel(tc, attn_weights, v, Wo, bo, out):
                     for t in range(PACK):
                         first = P * (PACK * g + t)
                         nc.tensor.transpose(turned[:, t, :], raw[:, first : first + P], ident_bf16[:])
-                    nc.scalar.copy(
+                    copy = nc.vector.tensor_copy if g == 1 and block % 2 == 1 else nc.scalar.copy
+                    copy(
                         out=grouped[:, g, P * block : P * (block + 1), :],
                         in_=turned[:].rearrange("p t f -> p f t"),
                     )
@@ -155,14 +168,13 @@ def tile_attention_pb_kernel(tc, attn_weights, v, Wo, bo, out):
         o_scales = {}
 
         def turn(step, pairs):
-            unit, j = divmod(step, ROWS_PER_PARTITION)
             if step not in a_grouped:
                 a_grouped[step] = ring.tile([P, HEADS * P * PACK], BF16, name="a_grouped", align_bytes=64)
             grouped = a_grouped[step]
             for pair in pairs:
                 turned = psum_turn.tile([P, 2, 2, P], F32, name="a_turned", tag="turned")
                 for i in range(2):
-                    words = a_raw[(unit, 2 * pair + i)][:, j, :].bitcast(F32)
+                    words = a_raw[(step, 2 * pair + i)].bitcast(F32)
                     for u in range(2):
                         nc.tensor.transpose(turned[:, i, u, :], words[:, P * u : P * (u + 1)], ident_f32[:])
                 width = 2 * P * PACK
@@ -245,6 +257,7 @@ def tile_attention_pb_kernel(tc, attn_weights, v, Wo, bo, out):
                 nc.sync.dma_start(out=rows[:, cols], in_=result[:, cols])
 
         early, late = range(HEADS // 4), range(HEADS // 4, HEADS // 2)
+        prepare_wo(0)
         for step in range(ROWS_PER_PARTITION):
             turn(step, early)
         regroup_v(0)
@@ -253,9 +266,8 @@ def tile_attention_pb_kernel(tc, attn_weights, v, Wo, bo, out):
             turn(step, late)
         for step in range(ROWS_PER_PARTITION):
             quantise_attn(step)
-        prepare_wo(0)
-        spread_bias()
         prepare_wo(1)
+        spread_bias()
         mix(0)
 
         for i in range(ROWS_PER_PARTITION, STEPS + 3):
@@ -271,6 +283,7 @@ def tile_attention_pb_kernel(tc, attn_weights, v, Wo, bo, out):
                 mix(i - 1)
             if 0 <= i - 3:
                 project(i - 3)
-            if i == 3:
+            if i == 2:
                 regroup_v(1)
+            if i == 3:
                 quantise_v(1)

@@ -36,16 +36,15 @@ def tile_attention_pb_kernel(tc, attn_weights, v, Wo, bo, out):
         psum_out = ctx.enter_context(tc.psum_pool(name="psum_out", bufs=2))
         ctx.enter_context(tc.manual_schedule())
 
-        ident_f32 = keep.tile([P, P], F32, name="ident_f32")
-        make_identity(nc, ident_f32[:])
-        ident_bf16 = keep.tile([P, P], BF16, name="ident_bf16")
-        make_identity(nc, ident_bf16[:])
+        bias_rows = keep.tile([P, FEATURES], BF16, name="bias_rows")
+        nc.vector.memset(bias_rows[:].bitcast(F32), 0.0)
         ones = keep.tile([P, P], BF16, name="ones")
         nc.vector.memset(ones[:], 1.0)
-        bias_rows = keep.tile([P, FEATURES], BF16, name="bias_rows")
-        nc.vector.memset(bias_rows[:], 0.0)
+        ident_bf16 = keep.tile([P, P], BF16, name="ident_bf16")
+        make_identity(nc, ident_bf16[:])
+        ident_f32 = keep.tile([P, P], F32, name="ident_f32")
+        make_identity(nc, ident_f32[:])
 
-        nc.scalar.dma_start(out=bias_rows[0:1, :], in_=bo.rearrange("(o e) -> o e", o=1))
 
         def load_wo(pair):
             raw = keep.tile([P, 2, FEATURES], BF16, name="wo_raw%d" % pair)
@@ -82,7 +81,9 @@ def tile_attention_pb_kernel(tc, attn_weights, v, Wo, bo, out):
             for h in range(heads):
                 a_raw[(step, first + h)] = raw[:, h, :]
 
-        wo_raw = [load_wo(0), load_wo(1)]
+        wo_raw = [load_wo(0)]
+        nc.sync.dma_start(out=bias_rows[0:1, :], in_=bo.rearrange("(o e) -> o e", o=1))
+        wo_raw.append(load_wo(1))
         load_unit(0, 0, 2)
         load_unit(0, 2, 2)
         v_raw = [load_v(0)]
@@ -123,19 +124,30 @@ def tile_attention_pb_kernel(tc, attn_weights, v, Wo, bo, out):
             v_codes.append(codes)
             v_scales.append(scales)
 
+        bias = keep.tile([P, FEATURES], F32, name="bias")
+
+        def spread_bias():
+            for half in range(HALVES):
+                cols = slice(BANK * half, BANK * (half + 1))
+                spread = psum_out.tile([P, BANK], F32, name="spread", tag="acc")
+                nc.tensor.matmul(out=spread[:], lhsT=ones[:], rhs=bias_rows[:, cols], start=True, stop=True)
+                nc.scalar.copy(out=bias[:, cols], in_=spread[:])
+
         wo_codes = []
         wo_scales = []
 
         def prepare_wo(half):
             grouped = ring.tile([P, PASSES, BANK, PACK], BF16, name="wo_grouped", align_bytes=64)
             for block in range(BANK // P):
+                if half == 0 and block == 2:
+                    spread_bias()
                 raw = wo_raw[2 * half + block // 2][:, block % 2, :]
                 for g in range(PASSES):
                     turned = psum_turn.tile([P, PACK, P], BF16, name="wo_turned", tag="turned")
                     for t in range(PACK):
                         first = P * (PACK * g + t)
                         nc.tensor.transpose(turned[:, t, :], raw[:, first : first + P], ident_bf16[:])
-                    copy = nc.vector.tensor_copy if g == 1 and block % 2 == 1 else nc.scalar.copy
+                    copy = nc.vector.tensor_copy if half == 0 and g == 1 else nc.scalar.copy
                     copy(
                         out=grouped[:, g, P * block : P * (block + 1), :],
                         in_=turned[:].rearrange("p t f -> p f t"),
@@ -149,15 +161,6 @@ def tile_attention_pb_kernel(tc, attn_weights, v, Wo, bo, out):
             )
             wo_codes.append(codes)
             wo_scales.append(scales)
-
-        bias = keep.tile([P, FEATURES], F32, name="bias")
-
-        def spread_bias():
-            for half in range(HALVES):
-                cols = slice(BANK * half, BANK * (half + 1))
-                spread = psum_out.tile([P, BANK], F32, name="spread", tag="acc")
-                nc.tensor.matmul(out=spread[:], lhsT=ones[:], rhs=bias_rows[:, cols], start=True, stop=True)
-                nc.vector.tensor_copy(out=bias[:, cols], in_=spread[:])
 
         a_grouped = {}
         a_codes = {}
@@ -267,7 +270,6 @@ def tile_attention_pb_kernel(tc, attn_weights, v, Wo, bo, out):
         for step in range(ROWS_PER_PARTITION):
             quantise_attn(step)
         prepare_wo(1)
-        spread_bias()
         mix(0)
 
         for i in range(ROWS_PER_PARTITION, STEPS + 3):

@@ -84,11 +84,9 @@ def tile_attention_pb_kernel(tc, attn_weights, v, Wo, bo, out):
         wo_raw = [load_wo(0)]
         nc.sync.dma_start(out=bias_rows[0:1, :], in_=bo.rearrange("(o e) -> o e", o=1))
         wo_raw.append(load_wo(1))
-        load_unit(0, 0, 2)
-        load_unit(0, 2, 2)
+        for first in range(0, HEADS, 2):
+            load_unit(0, first, 2)
         v_raw = [load_v(0)]
-        load_unit(0, 4, 2)
-        load_unit(0, 6, 2)
         wo_raw.extend([load_wo(2), load_wo(3)])
         for g in range(PASSES):
             load_unit(1, PACK * g, PACK)
@@ -139,15 +137,13 @@ def tile_attention_pb_kernel(tc, attn_weights, v, Wo, bo, out):
         def prepare_wo(half):
             grouped = ring.tile([P, PASSES, BANK, PACK], BF16, name="wo_grouped", align_bytes=64)
             for block in range(BANK // P):
-                if half == 0 and block == 2:
-                    spread_bias()
                 raw = wo_raw[2 * half + block // 2][:, block % 2, :]
                 for g in range(PASSES):
                     turned = psum_turn.tile([P, PACK, P], BF16, name="wo_turned", tag="turned")
                     for t in range(PACK):
                         first = P * (PACK * g + t)
                         nc.tensor.transpose(turned[:, t, :], raw[:, first : first + P], ident_bf16[:])
-                    copy = nc.vector.tensor_copy if half == 0 and g == 1 else nc.scalar.copy
+                    copy = nc.vector.tensor_copy if half == 0 and g == 1 and block % 2 == 1 else nc.scalar.copy
                     copy(
                         out=grouped[:, g, P * block : P * (block + 1), :],
                         in_=turned[:].rearrange("p t f -> p f t"),
@@ -261,6 +257,7 @@ def tile_attention_pb_kernel(tc, attn_weights, v, Wo, bo, out):
 
         early, late = range(HEADS // 4), range(HEADS // 4, HEADS // 2)
         prepare_wo(0)
+        spread_bias()
         for step in range(ROWS_PER_PARTITION):
             turn(step, early)
         regroup_v(0)
@@ -275,17 +272,17 @@ def tile_attention_pb_kernel(tc, attn_weights, v, Wo, bo, out):
         for i in range(ROWS_PER_PARTITION, STEPS + 3):
             if 0 <= i - 2 < STEPS:
                 round_mixed(i - 2)
-            if i < STEPS:
-                turn(i, range(HEADS // 2))
+            if ROWS_PER_PARTITION <= i - 1 < STEPS:
+                quantise_attn(i - 1)
+            if i == 3:
+                regroup_v(1)
             if 0 <= i - 2 < STEPS:
                 quantise_mixed(i - 2)
             if i < STEPS:
-                quantise_attn(i)
-            if 0 <= i - 1 < STEPS:
-                mix(i - 1)
+                turn(i, range(HEADS // 2))
             if 0 <= i - 3:
                 project(i - 3)
-            if i == 2:
-                regroup_v(1)
-            if i == 3:
+            if i == 4:
                 quantise_v(1)
+            if 0 <= i - 1 < STEPS:
+                mix(i - 1)

@@ -86,8 +86,9 @@ def tile_attention_pb_kernel(tc, attn_weights, v, Wo, bo, out):
         wo_raw.append(load_wo(1))
         for first in range(0, HEADS, 2):
             load_unit(0, first, 2)
+        wo_raw.append(load_wo(2))
         v_raw = [load_v(0)]
-        wo_raw.extend([load_wo(2), load_wo(3)])
+        wo_raw.append(load_wo(3))
         for g in range(PASSES):
             load_unit(1, PACK * g, PACK)
         v_raw.append(load_v(1))
@@ -137,6 +138,8 @@ def tile_attention_pb_kernel(tc, attn_weights, v, Wo, bo, out):
         def prepare_wo(half):
             grouped = ring.tile([P, PASSES, BANK, PACK], BF16, name="wo_grouped", align_bytes=64)
             for block in range(BANK // P):
+                if half == 0 and block == 2:
+                    spread_bias()
                 raw = wo_raw[2 * half + block // 2][:, block % 2, :]
                 for g in range(PASSES):
                     turned = psum_turn.tile([P, PACK, P], BF16, name="wo_turned", tag="turned")
@@ -166,7 +169,7 @@ def tile_attention_pb_kernel(tc, attn_weights, v, Wo, bo, out):
         o_codes = {}
         o_scales = {}
 
-        def turn(step, pairs):
+        def turn(step, pairs, vector_pair=None):
             if step not in a_grouped:
                 a_grouped[step] = ring.tile([P, HEADS * P * PACK], BF16, name="a_grouped", align_bytes=64)
             grouped = a_grouped[step]
@@ -177,7 +180,8 @@ def tile_attention_pb_kernel(tc, attn_weights, v, Wo, bo, out):
                     for u in range(2):
                         nc.tensor.transpose(turned[:, i, u, :], words[:, P * u : P * (u + 1)], ident_f32[:])
                 width = 2 * P * PACK
-                nc.scalar.copy(
+                copy = nc.vector.tensor_copy if pair == vector_pair else nc.scalar.copy
+                copy(
                     out=grouped[:, width * pair : width * (pair + 1)]
                     .bitcast(F32)
                     .rearrange("p (i n u) -> p i n u", i=2, u=2),
@@ -257,15 +261,14 @@ def tile_attention_pb_kernel(tc, attn_weights, v, Wo, bo, out):
 
         early, late = range(HEADS // 4), range(HEADS // 4, HEADS // 2)
         prepare_wo(0)
-        spread_bias()
-        for step in range(ROWS_PER_PARTITION):
-            turn(step, early)
-        regroup_v(0)
-        quantise_v(0)
+        turn(0, early)
+        turn(1, early, vector_pair=1)
         for step in range(ROWS_PER_PARTITION):
             turn(step, late)
         for step in range(ROWS_PER_PARTITION):
             quantise_attn(step)
+        regroup_v(0)
+        quantise_v(0)
         prepare_wo(1)
         mix(0)
 

@@ -22,6 +22,7 @@ ROWS_PER_PARTITION = 2
 UNIT_TOKENS = ROWS_PER_PARTITION * P
 UNITS = BATCHES * TOKENS // UNIT_TOKENS
 STEPS = UNITS * ROWS_PER_PARTITION
+WARM_UP = 4
 
 FLOPS = 2 * BATCHES * HEADS * TOKENS * TOKENS * P + 2 * BATCHES * TOKENS * FEATURES * FEATURES
 
@@ -36,10 +37,10 @@ def tile_attention_pb_kernel(tc, attn_weights, v, Wo, bo, out):
         psum_out = ctx.enter_context(tc.psum_pool(name="psum_out", bufs=2))
         ctx.enter_context(tc.manual_schedule())
 
+        ones = keep.tile([P, BANK], BF16, name="ones")
+        nc.vector.memset(ones[:], 1.0)
         bias_rows = keep.tile([P, FEATURES], BF16, name="bias_rows")
         nc.vector.memset(bias_rows[:].bitcast(F32), 0.0)
-        ones = keep.tile([P, P], BF16, name="ones")
-        nc.vector.memset(ones[:], 1.0)
         ident_bf16 = keep.tile([P, P], BF16, name="ident_bf16")
         make_identity(nc, ident_bf16[:])
         ident_f32 = keep.tile([P, P], F32, name="ident_f32")
@@ -52,13 +53,15 @@ def tile_attention_pb_kernel(tc, attn_weights, v, Wo, bo, out):
             nc.sync.dma_start(out=raw[:], in_=rows.rearrange("(r p) e -> p r e", p=P))
             return raw
 
-        def load_v(b):
-            raw = keep.tile([P, PACK, FEATURES], BF16, name="v_raw%d" % b)
-            nc.sync.dma_start(
-                out=raw[:].rearrange("p (u e) c -> p u e c", u=2),
-                in_=v[b].rearrange("(u p e) h d -> p u e (h d)", u=2, e=2),
-            )
-            return raw
+        v_raw = {}
+
+        def load_v(b, first, heads):
+            raw = keep.tile([P, PACK, heads * P], BF16, name="v_raw%d_%d" % (b, first))
+            rows = v[b][:, first : first + heads, :].rearrange("(u p e) h d -> u p e (h d)", u=2, e=2)
+            for u in range(2):
+                nc.sync.dma_start(out=raw[:, 2 * u : 2 * (u + 1), :], in_=rows[u])
+            for g in range(heads // PACK):
+                v_raw[(b, first // PACK + g)] = raw[:, :, BANK * g : BANK * (g + 1)]
 
         a_raw = {}
 
@@ -81,47 +84,43 @@ def tile_attention_pb_kernel(tc, attn_weights, v, Wo, bo, out):
             for h in range(heads):
                 a_raw[(step, first + h)] = raw[:, h, :]
 
-        wo_raw = [load_wo(0)]
-        nc.sync.dma_start(out=bias_rows[0:1, :], in_=bo.rearrange("(o e) -> o e", o=1))
-        wo_raw.append(load_wo(1))
+        wo_raw = [load_wo(0), load_wo(1)]
         for first in range(0, HEADS, 2):
             load_unit(0, first, 2)
+        nc.sync.dma_start(out=bias_rows[0:1, :], in_=bo.rearrange("(o e) -> o e", o=1))
         wo_raw.append(load_wo(2))
-        v_raw = [load_v(0)]
+        load_v(0, 0, HEADS)
         wo_raw.append(load_wo(3))
-        for g in range(PASSES):
-            load_unit(1, PACK * g, PACK)
-        v_raw.append(load_v(1))
-        for step in range(STEPS // 2, STEPS):
+        for step in range(ROWS_PER_PARTITION, STEPS):
             for g in range(PASSES):
                 load_step(step, PACK * g, PACK)
+            if step == 2:
+                load_v(1, 0, PACK)
+            if step == 4:
+                load_v(1, PACK, PACK)
 
-        v_codes = []
-        v_scales = []
+        v_grouped = {}
+        v_codes = {}
+        v_scales = {}
 
-        v_grouped = []
-        halves = [slice(BANK * s, BANK * (s + 1)) for s in range(HALVES)]
+        def regroup_v(b, g):
+            grouped = keep.tile([P, BANK, PACK], BF16, name="v_grouped%d" % g, align_bytes=64)
+            nc.vector.tensor_copy(
+                out=grouped[:].rearrange("p (c i) t -> p c t i", i=4),
+                in_=v_raw[(b, g)].rearrange("p t (c i) -> p c t i", i=4),
+            )
+            v_grouped[(b, g)] = grouped
 
-        def regroup_v(b):
-            grouped = keep.tile([P, FEATURES, PACK], BF16, name="v_grouped", align_bytes=64)
-            for cols in halves:
-                nc.vector.tensor_copy(
-                    out=grouped[:, cols, :].rearrange("p (c i) t -> p c t i", i=4),
-                    in_=v_raw[b][:, :, cols].rearrange("p t (c i) -> p c t i", i=4),
-                )
-            v_grouped.append(grouped)
-
-        def quantise_v(b):
-            codes = keep.tile([P, FEATURES], U32, name="v_codes%d" % b, align_bytes=64)
-            scales = keep.tile([P, FEATURES], U8, name="v_scales%d" % b, align_bytes=64)
-            for cols in halves:
-                nc.vector.quantize_mx(
-                    out=codes[:, cols].bitcast(FP8X4),
-                    scales=scales[:, cols],
-                    in_=v_grouped[b][:, cols, :].rearrange("p c t -> p (c t)"),
-                )
-            v_codes.append(codes)
-            v_scales.append(scales)
+        def quantise_v(b, g):
+            codes = keep.tile([P, BANK], U32, name="v_codes%d_%d" % (b, g), align_bytes=64)
+            scales = keep.tile([P, BANK], U8, name="v_scales%d_%d" % (b, g), align_bytes=64)
+            nc.vector.quantize_mx(
+                out=codes[:].bitcast(FP8X4),
+                scales=scales[:],
+                in_=v_grouped[(b, g)][:].rearrange("p c t -> p (c t)"),
+            )
+            v_codes[(b, g)] = codes
+            v_scales[(b, g)] = scales
 
         bias = keep.tile([P, FEATURES], F32, name="bias")
 
@@ -129,8 +128,8 @@ def tile_attention_pb_kernel(tc, attn_weights, v, Wo, bo, out):
             for half in range(HALVES):
                 cols = slice(BANK * half, BANK * (half + 1))
                 spread = psum_out.tile([P, BANK], F32, name="spread", tag="acc")
-                nc.tensor.matmul(out=spread[:], lhsT=ones[:], rhs=bias_rows[:, cols], start=True, stop=True)
-                nc.scalar.copy(out=bias[:, cols], in_=spread[:])
+                nc.tensor.matmul(out=spread[:], lhsT=ones[:, 0:P], rhs=bias_rows[:, cols], start=True, stop=True)
+                nc.vector.tensor_copy(out=bias[:, cols], in_=spread[:])
 
         wo_codes = []
         wo_scales = []
@@ -138,15 +137,19 @@ def tile_attention_pb_kernel(tc, attn_weights, v, Wo, bo, out):
         def prepare_wo(half):
             grouped = ring.tile([P, PASSES, BANK, PACK], BF16, name="wo_grouped", align_bytes=64)
             for block in range(BANK // P):
-                if half == 0 and block == 2:
-                    spread_bias()
                 raw = wo_raw[2 * half + block // 2][:, block % 2, :]
                 for g in range(PASSES):
                     turned = psum_turn.tile([P, PACK, P], BF16, name="wo_turned", tag="turned")
                     for t in range(PACK):
                         first = P * (PACK * g + t)
-                        nc.tensor.transpose(turned[:, t, :], raw[:, first : first + P], ident_bf16[:])
-                    copy = nc.vector.tensor_copy if half == 0 and g == 1 and block % 2 == 1 else nc.scalar.copy
+                        block_in = raw[:, first : first + P]
+                        if half == 0:
+                            nc.tensor.matmul(
+                                out=turned[:, t, :], lhsT=block_in, rhs=ident_bf16[:], start=True, stop=True
+                            )
+                        else:
+                            nc.tensor.transpose(turned[:, t, :], block_in, ident_bf16[:])
+                    copy = nc.vector.tensor_copy if half == 0 and g == 1 else nc.scalar.copy
                     copy(
                         out=grouped[:, g, P * block : P * (block + 1), :],
                         in_=turned[:].rearrange("p t f -> p f t"),
@@ -191,12 +194,13 @@ def tile_attention_pb_kernel(tc, attn_weights, v, Wo, bo, out):
         def quantise_attn(step):
             codes = ring.tile([P, HEADS * P], U32, name="a_codes", align_bytes=64)
             scales = ring.tile([P, HEADS * P], U8, name="a_scales", align_bytes=64)
-            for g in range(PASSES):
-                cols = slice(PACK * P * g, PACK * P * (g + 1))
+            width = 2 * P
+            for pair in range(HEADS // 2):
+                cols = slice(width * pair, width * (pair + 1))
                 nc.vector.quantize_mx(
                     out=codes[:, cols].bitcast(FP8X4),
                     scales=scales[:, cols],
-                    in_=a_grouped[step][:, PACK * PACK * P * g : PACK * PACK * P * (g + 1)],
+                    in_=a_grouped[step][:, PACK * width * pair : PACK * width * (pair + 1)],
                 )
             a_codes[step] = codes
             a_scales[step] = scales
@@ -208,10 +212,11 @@ def tile_attention_pb_kernel(tc, attn_weights, v, Wo, bo, out):
                 bank = psum_mix.tile([P, PACK, P], F32, name="o_turned")
                 for t in range(PACK):
                     cols = slice(P * (PACK * g + t), P * (PACK * g + t + 1))
+                    v_cols = slice(P * t, P * (t + 1))
                     nc.tensor.matmul_mx(
                         out=bank[:, t, :],
-                        lhsT=v_codes[b][:, cols].bitcast(FP8X4),
-                        lhsT_scale=v_scales[b][:, cols],
+                        lhsT=v_codes[(b, g)][:, v_cols].bitcast(FP8X4),
+                        lhsT_scale=v_scales[(b, g)][:, v_cols],
                         rhs=a_codes[step][:, cols].bitcast(FP8X4),
                         rhs_scale=a_scales[step][:, cols],
                         start=True,
@@ -237,12 +242,9 @@ def tile_attention_pb_kernel(tc, attn_weights, v, Wo, bo, out):
             o_codes[step] = codes
             o_scales[step] = scales
 
+        accs = {}
+
         def project(step):
-            unit, j = divmod(step, ROWS_PER_PARTITION)
-            b, part = divmod(unit, UNITS // BATCHES)
-            rows = out[b, UNIT_TOKENS * part : UNIT_TOKENS * (part + 1)]
-            rows = rows.rearrange("(p j) a d -> p j (a d)", j=ROWS_PER_PARTITION)[:, j, :]
-            result = keep.tile([P, FEATURES], F32, name="result%d" % step)
             for half in range(HALVES):
                 acc = psum_out.tile([P, BANK], F32, name="acc", tag="acc")
                 for g in range(PASSES):
@@ -255,10 +257,24 @@ def tile_attention_pb_kernel(tc, attn_weights, v, Wo, bo, out):
                         start=(g == 0),
                         stop=(g == PASSES - 1),
                     )
+                accs[(step, half)] = acc
+
+        def add_bias(step):
+            unit, j = divmod(step, ROWS_PER_PARTITION)
+            b, part = divmod(unit, UNITS // BATCHES)
+            rows = out[b, UNIT_TOKENS * part : UNIT_TOKENS * (part + 1)]
+            rows = rows.rearrange("(p j) a d -> p j (a d)", j=ROWS_PER_PARTITION)[:, j, :]
+            result = keep.tile([P, FEATURES], F32, name="result%d" % step)
+            for half in range(HALVES):
                 cols = slice(BANK * half, BANK * (half + 1))
-                nc.vector.tensor_tensor(out=result[:, cols], in0=acc[:], in1=bias[:, cols], op=mybir.AluOpType.add)
+                nc.vector.tensor_tensor(
+                    out=result[:, cols], in0=accs[(step, half)][:], in1=bias[:, cols], op=mybir.AluOpType.add
+                )
                 nc.sync.dma_start(out=rows[:, cols], in_=result[:, cols])
 
+        warm = psum_out.tile([P, BANK], F32, name="warm", tag="acc")
+        for n in range(WARM_UP):
+            nc.tensor.matmul(out=warm[:], lhsT=ones[:, 0:P], rhs=ones[:], start=True, stop=True)
         early, late = range(HEADS // 4), range(HEADS // 4, HEADS // 2)
         prepare_wo(0)
         turn(0, early)
@@ -267,25 +283,34 @@ def tile_attention_pb_kernel(tc, attn_weights, v, Wo, bo, out):
             turn(step, late)
         for step in range(ROWS_PER_PARTITION):
             quantise_attn(step)
-        regroup_v(0)
-        quantise_v(0)
+        for g in range(PASSES):
+            regroup_v(0, g)
+        for g in range(PASSES):
+            quantise_v(0, g)
         prepare_wo(1)
+        spread_bias()
         mix(0)
 
         for i in range(ROWS_PER_PARTITION, STEPS + 3):
-            if 0 <= i - 2 < STEPS:
+            if i - 2 < STEPS:
                 round_mixed(i - 2)
-            if ROWS_PER_PARTITION <= i - 1 < STEPS:
-                quantise_attn(i - 1)
-            if i == 3:
-                regroup_v(1)
-            if 0 <= i - 2 < STEPS:
-                quantise_mixed(i - 2)
             if i < STEPS:
                 turn(i, range(HEADS // 2))
+            if i == 3:
+                regroup_v(1, 0)
+            if ROWS_PER_PARTITION <= i - 1 < STEPS:
+                quantise_attn(i - 1)
+            if i == 5:
+                quantise_v(1, 1)
             if 0 <= i - 3:
                 project(i - 3)
             if i == 4:
-                quantise_v(1)
-            if 0 <= i - 1 < STEPS:
+                quantise_v(1, 0)
+            if i - 2 < STEPS:
+                quantise_mixed(i - 2)
+            if i == 4:
+                regroup_v(1, 1)
+            if 0 <= i - 3:
+                add_bias(i - 3)
+            if i - 1 < STEPS:
                 mix(i - 1)

@@ -85,9 +85,9 @@ def tile_attention_pb_kernel(tc, attn_weights, v, Wo, bo, out):
                 a_raw[(step, first + h)] = raw[:, h, :]
 
         wo_raw = [load_wo(0), load_wo(1)]
+        nc.sync.dma_start(out=bias_rows[0:1, :], in_=bo.rearrange("(o e) -> o e", o=1))
         for first in range(0, HEADS, 2):
             load_unit(0, first, 2)
-        nc.sync.dma_start(out=bias_rows[0:1, :], in_=bo.rearrange("(o e) -> o e", o=1))
         wo_raw.append(load_wo(2))
         load_v(0, 0, HEADS)
         wo_raw.append(load_wo(3))
@@ -137,9 +137,13 @@ def tile_attention_pb_kernel(tc, attn_weights, v, Wo, bo, out):
         def prepare_wo(half):
             grouped = ring.tile([P, PASSES, BANK, PACK], BF16, name="wo_grouped", align_bytes=64)
             for block in range(BANK // P):
+                if half == 0 and block == 2:
+                    spread_bias()
                 raw = wo_raw[2 * half + block // 2][:, block % 2, :]
                 for g in range(PASSES):
-                    turned = psum_turn.tile([P, PACK, P], BF16, name="wo_turned", tag="turned")
+                    by_vector = half == 0 and g == 1
+                    pool, tag = (psum_mix, "mixed") if by_vector else (psum_turn, "turned")
+                    turned = pool.tile([P, PACK, P], BF16, name="wo_turned", tag=tag)
                     for t in range(PACK):
                         first = P * (PACK * g + t)
                         block_in = raw[:, first : first + P]
@@ -149,7 +153,7 @@ def tile_attention_pb_kernel(tc, attn_weights, v, Wo, bo, out):
                             )
                         else:
                             nc.tensor.transpose(turned[:, t, :], block_in, ident_bf16[:])
-                    copy = nc.vector.tensor_copy if half == 0 and g == 1 else nc.scalar.copy
+                    copy = nc.vector.tensor_copy if by_vector else nc.scalar.copy
                     copy(
                         out=grouped[:, g, P * block : P * (block + 1), :],
                         in_=turned[:].rearrange("p t f -> p f t"),
@@ -172,7 +176,7 @@ def tile_attention_pb_kernel(tc, attn_weights, v, Wo, bo, out):
         o_codes = {}
         o_scales = {}
 
-        def turn(step, pairs, vector_pair=None):
+        def turn(step, pairs):
             if step not in a_grouped:
                 a_grouped[step] = ring.tile([P, HEADS * P * PACK], BF16, name="a_grouped", align_bytes=64)
             grouped = a_grouped[step]
@@ -183,8 +187,7 @@ def tile_attention_pb_kernel(tc, attn_weights, v, Wo, bo, out):
                     for u in range(2):
                         nc.tensor.transpose(turned[:, i, u, :], words[:, P * u : P * (u + 1)], ident_f32[:])
                 width = 2 * P * PACK
-                copy = nc.vector.tensor_copy if pair == vector_pair else nc.scalar.copy
-                copy(
+                nc.scalar.copy(
                     out=grouped[:, width * pair : width * (pair + 1)]
                     .bitcast(F32)
                     .rearrange("p (i n u) -> p i n u", i=2, u=2),
@@ -209,7 +212,7 @@ def tile_attention_pb_kernel(tc, attn_weights, v, Wo, bo, out):
             b = step // (STEPS // BATCHES)
             banks = []
             for g in range(PASSES):
-                bank = psum_mix.tile([P, PACK, P], F32, name="o_turned")
+                bank = psum_mix.tile([P, PACK, P], F32, name="o_turned", tag="mixed")
                 for t in range(PACK):
                     cols = slice(P * (PACK * g + t), P * (PACK * g + t + 1))
                     v_cols = slice(P * t, P * (t + 1))
@@ -246,7 +249,10 @@ def tile_attention_pb_kernel(tc, attn_weights, v, Wo, bo, out):
 
         def project(step):
             for half in range(HALVES):
-                acc = psum_out.tile([P, BANK], F32, name="acc", tag="acc")
+                if step < STEPS - 3:
+                    acc = psum_out.tile([P, BANK], F32, name="acc", tag="acc")
+                else:
+                    acc = psum_turn.tile([P, BANK], F32, name="acc_late", tag="turned")
                 for g in range(PASSES):
                     nc.tensor.matmul_mx(
                         out=acc[:],
@@ -266,21 +272,26 @@ def tile_attention_pb_kernel(tc, attn_weights, v, Wo, bo, out):
             rows = rows.rearrange("(p j) a d -> p j (a d)", j=ROWS_PER_PARTITION)[:, j, :]
             result = keep.tile([P, FEATURES], F32, name="result%d" % step)
             for half in range(HALVES):
-                cols = slice(BANK * half, BANK * (half + 1))
-                nc.vector.tensor_tensor(
-                    out=result[:, cols], in0=accs[(step, half)][:], in1=bias[:, cols], op=mybir.AluOpType.add
-                )
-                nc.sync.dma_start(out=rows[:, cols], in_=result[:, cols])
+                pieces = 2 if step == STEPS - 1 and half == HALVES - 1 else 1
+                width = BANK // pieces
+                for piece in range(pieces):
+                    cols = slice(BANK * half + width * piece, BANK * half + width * (piece + 1))
+                    nc.vector.tensor_tensor(
+                        out=result[:, cols],
+                        in0=accs[(step, half)][:, width * piece : width * (piece + 1)],
+                        in1=bias[:, cols],
+                        op=mybir.AluOpType.add,
+                    )
+                    nc.sync.dma_start(out=rows[:, cols], in_=result[:, cols])
 
         warm = psum_out.tile([P, BANK], F32, name="warm", tag="acc")
         for n in range(WARM_UP):
             nc.tensor.matmul(out=warm[:], lhsT=ones[:, 0:P], rhs=ones[:], start=True, stop=True)
         early, late = range(HEADS // 4), range(HEADS // 4, HEADS // 2)
         prepare_wo(0)
-        turn(0, early)
-        turn(1, early, vector_pair=1)
-        for step in range(ROWS_PER_PARTITION):
-            turn(step, late)
+        for pairs in (early, late):
+            for step in range(ROWS_PER_PARTITION):
+                turn(step, pairs)
         for step in range(ROWS_PER_PARTITION):
             quantise_attn(step)
         for g in range(PASSES):
@@ -288,7 +299,6 @@ def tile_attention_pb_kernel(tc, attn_weights, v, Wo, bo, out):
         for g in range(PASSES):
             quantise_v(0, g)
         prepare_wo(1)
-        spread_bias()
         mix(0)
 
         for i in range(ROWS_PER_PARTITION, STEPS + 3):

from contextlib import ExitStack

import concourse.mybir as mybir
from concourse.masks import make_identity

BF16 = mybir.dt.bfloat16
F32 = mybir.dt.float32
U32 = mybir.dt.uint32
U8 = mybir.dt.uint8
FP8X4 = mybir.dt.float8_e4m3fn_x4

P = 128
PACK = 4
BATCHES = 2
TOKENS = 512
HEADS = 8
FEATURES = HEADS * P
BANK = 512
PASSES = FEATURES // (P * PACK)
HALVES = FEATURES // BANK
ROWS_PER_PARTITION = 2
UNIT_TOKENS = ROWS_PER_PARTITION * P
UNITS = BATCHES * TOKENS // UNIT_TOKENS
STEPS = UNITS * ROWS_PER_PARTITION
WARM_UP = 4

FLOPS = 2 * BATCHES * HEADS * TOKENS * TOKENS * P + 2 * BATCHES * TOKENS * FEATURES * FEATURES


def tile_attention_pb_kernel(tc, attn_weights, v, Wo, bo, out):
    nc = tc.nc
    with ExitStack() as ctx:
        keep = ctx.enter_context(tc.tile_pool(name="keep", bufs=1))
        ring = ctx.enter_context(tc.tile_pool(name="ring", bufs=2))
        psum_turn = ctx.enter_context(tc.psum_pool(name="psum_turn", bufs=4))
        psum_mix = ctx.enter_context(tc.psum_pool(name="psum_mix", bufs=2))
        psum_out = ctx.enter_context(tc.psum_pool(name="psum_out", bufs=2))
        ctx.enter_context(tc.manual_schedule())

        ones = keep.tile([P, BANK], BF16, name="ones")
        nc.vector.memset(ones[:], 1.0)
        bias_rows = keep.tile([P, FEATURES], BF16, name="bias_rows")
        nc.vector.memset(bias_rows[:].bitcast(F32), 0.0)
        ident_bf16 = keep.tile([P, P], BF16, name="ident_bf16")
        make_identity(nc, ident_bf16[:])
        ident_f32 = keep.tile([P, P], F32, name="ident_f32")
        make_identity(nc, ident_f32[:])


        def load_wo(pair):
            raw = keep.tile([P, 2, FEATURES], BF16, name="wo_raw%d" % pair)
            rows = Wo[2 * P * pair : 2 * P * (pair + 1), :]
            nc.sync.dma_start(out=raw[:], in_=rows.rearrange("(r p) e -> p r e", p=P))
            return raw

        v_raw = {}

        def load_v(b, first, heads):
            raw = keep.tile([P, PACK, heads * P], BF16, name="v_raw%d_%d" % (b, first))
            rows = v[b][:, first : first + heads, :].rearrange("(u p e) h d -> u p e (h d)", u=2, e=2)
            for u in range(2):
                nc.sync.dma_start(out=raw[:, 2 * u : 2 * (u + 1), :], in_=rows[u])
            for g in range(heads // PACK):
                v_raw[(b, first // PACK + g)] = raw[:, :, BANK * g : BANK * (g + 1)]

        a_raw = {}

        def attn_rows(unit, first, heads):
            b, part = divmod(unit, UNITS // BATCHES)
            rows = attn_weights[b, first : first + heads, UNIT_TOKENS * part : UNIT_TOKENS * (part + 1), :]
            return rows.rearrange("h (p j) k -> p h j k", j=ROWS_PER_PARTITION)

        def load_unit(unit, first, heads):
            raw = keep.tile([P, heads, ROWS_PER_PARTITION, TOKENS], BF16, name="a_raw%d_%d" % (unit, first))
            nc.sync.dma_start(out=raw[:], in_=attn_rows(unit, first, heads))
            for h in range(heads):
                for j in range(ROWS_PER_PARTITION):
                    a_raw[(ROWS_PER_PARTITION * unit + j, first + h)] = raw[:, h, j, :]

        def load_step(step, first, heads):
            unit, j = divmod(step, ROWS_PER_PARTITION)
            raw = keep.tile([P, heads, TOKENS], BF16, name="a_step%d_%d" % (step, first))
            nc.sync.dma_start(out=raw[:], in_=attn_rows(unit, first, heads)[:, :, j, :])
            for h in range(heads):
                a_raw[(step, first + h)] = raw[:, h, :]

        wo_raw = [load_wo(0), load_wo(1)]
        nc.sync.dma_start(out=bias_rows[0:1, :], in_=bo.rearrange("(o e) -> o e", o=1))
        for first in range(0, HEADS, 2):
            load_unit(0, first, 2)
        wo_raw.append(load_wo(2))
        load_v(0, 0, HEADS)
        wo_raw.append(load_wo(3))
        for step in range(ROWS_PER_PARTITION, STEPS):
            for g in range(PASSES):
                load_step(step, PACK * g, PACK)
            if step == 2:
                load_v(1, 0, PACK)
            if step == 4:
                load_v(1, PACK, PACK)

        v_grouped = {}
        v_codes = {}
        v_scales = {}

        def regroup_v(b, g):
            grouped = keep.tile([P, BANK, PACK], BF16, name="v_grouped%d" % g, align_bytes=64)
            nc.vector.tensor_copy(
                out=grouped[:].rearrange("p (c i) t -> p c t i", i=4),
                in_=v_raw[(b, g)].rearrange("p t (c i) -> p c t i", i=4),
            )
            v_grouped[(b, g)] = grouped

        def quantise_v(b, g):
            codes = keep.tile([P, BANK], U32, name="v_codes%d_%d" % (b, g), align_bytes=64)
            scales = keep.tile([P, BANK], U8, name="v_scales%d_%d" % (b, g), align_bytes=64)
            nc.vector.quantize_mx(
                out=codes[:].bitcast(FP8X4),
                scales=scales[:],
                in_=v_grouped[(b, g)][:].rearrange("p c t -> p (c t)"),
            )
            v_codes[(b, g)] = codes
            v_scales[(b, g)] = scales

        bias = keep.tile([P, FEATURES], F32, name="bias")

        def spread_bias():
            for half in range(HALVES):
                cols = slice(BANK * half, BANK * (half + 1))
                spread = psum_out.tile([P, BANK], F32, name="spread", tag="acc")
                nc.tensor.matmul(out=spread[:], lhsT=ones[:, 0:P], rhs=bias_rows[:, cols], start=True, stop=True)
                nc.vector.tensor_copy(out=bias[:, cols], in_=spread[:])

        wo_codes = []
        wo_scales = []

        def prepare_wo(half):
            grouped = ring.tile([P, PASSES, BANK, PACK], BF16, name="wo_grouped", align_bytes=64)
            for block in range(BANK // P):
                if half == 0 and block == 2:
                    spread_bias()
                raw = wo_raw[2 * half + block // 2][:, block % 2, :]
                for g in range(PASSES):
                    by_vector = half == 0 and g == 1
                    pool, tag = (psum_mix, "mixed") if by_vector else (psum_turn, "turned")
                    turned = pool.tile([P, PACK, P], BF16, name="wo_turned", tag=tag)
                    for t in range(PACK):
                        first = P * (PACK * g + t)
                        block_in = raw[:, first : first + P]
                        if half == 0:
                            nc.tensor.matmul(
                                out=turned[:, t, :], lhsT=block_in, rhs=ident_bf16[:], start=True, stop=True
                            )
                        else:
                            nc.tensor.transpose(turned[:, t, :], block_in, ident_bf16[:])
                    copy = nc.vector.tensor_copy if by_vector else nc.scalar.copy
                    copy(
                        out=grouped[:, g, P * block : P * (block + 1), :],
                        in_=turned[:].rearrange("p t f -> p f t"),
                    )
            codes = keep.tile([P, PASSES * BANK], U32, name="wo_codes%d" % half, align_bytes=64)
            scales = keep.tile([P, PASSES * BANK], U8, name="wo_scales%d" % half, align_bytes=64)
            nc.vector.quantize_mx(
                out=codes[:].bitcast(FP8X4),
                scales=scales[:],
                in_=grouped[:].rearrange("p g f t -> p (g f t)"),
            )
            wo_codes.append(codes)
            wo_scales.append(scales)

        a_grouped = {}
        a_codes = {}
        a_scales = {}
        mixed = {}
        o_grouped = {}
        o_codes = {}
        o_scales = {}

        def turn(step, pairs):
            if step not in a_grouped:
                a_grouped[step] = ring.tile([P, HEADS * P * PACK], BF16, name="a_grouped", align_bytes=64)
            grouped = a_grouped[step]
            for pair in pairs:
                turned = psum_turn.tile([P, 2, 2, P], F32, name="a_turned", tag="turned")
                for i in range(2):
                    words = a_raw[(step, 2 * pair + i)].bitcast(F32)
                    for u in range(2):
                        nc.tensor.transpose(turned[:, i, u, :], words[:, P * u : P * (u + 1)], ident_f32[:])
                width = 2 * P * PACK
                nc.scalar.copy(
                    out=grouped[:, width * pair : width * (pair + 1)]
                    .bitcast(F32)
                    .rearrange("p (i n u) -> p i n u", i=2, u=2),
                    in_=turned[:].rearrange("p i u n -> p i n u"),
                )

        def quantise_attn(step):
            codes = ring.tile([P, HEADS * P], U32, name="a_codes", align_bytes=64)
            scales = ring.tile([P, HEADS * P], U8, name="a_scales", align_bytes=64)
            width = 2 * P
            for pair in range(HEADS // 2):
                cols = slice(width * pair, width * (pair + 1))
                nc.vector.quantize_mx(
                    out=codes[:, cols].bitcast(FP8X4),
                    scales=scales[:, cols],
                    in_=a_grouped[step][:, PACK * width * pair : PACK * width * (pair + 1)],
                )
            a_codes[step] = codes
            a_scales[step] = scales

        def mix(step):
            b = step // (STEPS // BATCHES)
            banks = []
            for g in range(PASSES):
                bank = psum_mix.tile([P, PACK, P], F32, name="o_turned", tag="mixed")
                for t in range(PACK):
                    cols = slice(P * (PACK * g + t), P * (PACK * g + t + 1))
                    v_cols = slice(P * t, P * (t + 1))
                    nc.tensor.matmul_mx(
                        out=bank[:, t, :],
                        lhsT=v_codes[(b, g)][:, v_cols].bitcast(FP8X4),
                        lhsT_scale=v_scales[(b, g)][:, v_cols],
                        rhs=a_codes[step][:, cols].bitcast(FP8X4),
                        rhs_scale=a_scales[step][:, cols],
                        start=True,
                        stop=True,
                    )
                banks.append(bank)
            mixed[step] = banks

        def round_mixed(step):
            grouped = ring.tile([P, PASSES, P, PACK], BF16, name="o_grouped", align_bytes=64)
            for g in range(PASSES):
                nc.scalar.copy(out=grouped[:, g, :, :], in_=mixed[step][g][:].rearrange("p t n -> p n t"))
            o_grouped[step] = grouped

        def quantise_mixed(step):
            codes = ring.tile([P, PASSES * P], U32, name="o_codes", align_bytes=64)
            scales = ring.tile([P, PASSES * P], U8, name="o_scales", align_bytes=64)
            nc.vector.quantize_mx(
                out=codes[:].bitcast(FP8X4),
                scales=scales[:],
                in_=o_grouped[step][:].rearrange("p g n t -> p (g n t)"),
            )
            o_codes[step] = codes
            o_scales[step] = scales

        accs = {}

        def project(step):
            for half in range(HALVES):
                if step < STEPS - 3:
                    acc = psum_out.tile([P, BANK], F32, name="acc", tag="acc")
                else:
                    acc = psum_turn.tile([P, BANK], F32, name="acc_late", tag="turned")
                for g in range(PASSES):
                    nc.tensor.matmul_mx(
                        out=acc[:],
                        lhsT=o_codes[step][:, P * g : P * (g + 1)].bitcast(FP8X4),
                        lhsT_scale=o_scales[step][:, P * g : P * (g + 1)],
                        rhs=wo_codes[half][:, BANK * g : BANK * (g + 1)].bitcast(FP8X4),
                        rhs_scale=wo_scales[half][:, BANK * g : BANK * (g + 1)],
                        start=(g == 0),
                        stop=(g == PASSES - 1),
                    )
                accs[(step, half)] = acc

        def add_bias(step):
            unit, j = divmod(step, ROWS_PER_PARTITION)
            b, part = divmod(unit, UNITS // BATCHES)
            rows = out[b, UNIT_TOKENS * part : UNIT_TOKENS * (part + 1)]
            rows = rows.rearrange("(p j) a d -> p j (a d)", j=ROWS_PER_PARTITION)[:, j, :]
            result = keep.tile([P, FEATURES], F32, name="result%d" % step)
            for half in range(HALVES):
                pieces = 2 if step == STEPS - 1 and half == HALVES - 1 else 1
                width = BANK // pieces
                for piece in range(pieces):
                    cols = slice(BANK * half + width * piece, BANK * half + width * (piece + 1))
                    nc.vector.tensor_tensor(
                        out=result[:, cols],
                        in0=accs[(step, half)][:, width * piece : width * (piece + 1)],
                        in1=bias[:, cols],
                        op=mybir.AluOpType.add,
                    )
                    nc.sync.dma_start(out=rows[:, cols], in_=result[:, cols])

        warm = psum_out.tile([P, BANK], F32, name="warm", tag="acc")
        for n in range(WARM_UP):
            nc.tensor.matmul(out=warm[:], lhsT=ones[:, 0:P], rhs=ones[:], start=True, stop=True)
        early, late = range(HEADS // 4), range(HEADS // 4, HEADS // 2)
        prepare_wo(0)
        for pairs in (early, late):
            for step in range(ROWS_PER_PARTITION):
                turn(step, pairs)
        for step in range(ROWS_PER_PARTITION):
            quantise_attn(step)
        for g in range(PASSES):
            regroup_v(0, g)
        for g in range(PASSES):
            quantise_v(0, g)
        prepare_wo(1)
        mix(0)

        for i in range(ROWS_PER_PARTITION, STEPS + 3):
            if i - 2 < STEPS:
                round_mixed(i - 2)
            if i < STEPS:
                turn(i, range(HEADS // 2))
            if i == 3:
                regroup_v(1, 0)
            if ROWS_PER_PARTITION <= i - 1 < STEPS:
                quantise_attn(i - 1)
            if i == 5:
                quantise_v(1, 1)
            if 0 <= i - 3:
                project(i - 3)
            if i == 4:
                quantise_v(1, 0)
            if i - 2 < STEPS:
                quantise_mixed(i - 2)
            if i == 4:
                regroup_v(1, 1)
            if 0 <= i - 3:
                add_bias(i - 3)
            if i - 1 < STEPS:
                mix(i - 1)
